import numpy as np
import ml_dtypes

BF16 = ml_dtypes.bfloat16


def bf(x):
    return np.asarray(x, np.float32).astype(BF16)


def f32(x):
    return np.asarray(x, np.float32)


def f64(x):
    return np.asarray(x).astype(np.float64)


def striped(idx):
    return np.tile(idx.reshape(-1, 16).T, (8, 1))


B, O, D, S, N = 24, 16, 512, 4096, 6144


def wdraw():
    return bf(np.random.standard_normal((D, D)) / np.sqrt(D))


def layer(x, rel, wa, ba, wb, bb):
    p = (rel.reshape(D, B, O, O) * x.reshape(D, B, O)[:, :, None, :]).reshape(D, N)
    msg = wb.T @ p + bb
    agg = msg.reshape(D, B, O * O).sum(axis=-1) / O
    return np.tanh(wa.T @ x + ba + np.repeat(agg, O, axis=-1) + x)


def setup_inputs():
    return {
        "table": f32(np.random.standard_normal((D, S))),
        "x0": f32(0.5 * np.random.standard_normal((D, O))),
        "w0": wdraw(),
        "b0": f32(0.1 * np.random.standard_normal((D, 1))),
        "w1": wdraw(),
        "b1": f32(0.5 / O * np.random.standard_normal((D, 1))),
        "w2": wdraw(),
        "b2": f32(0.1 * np.random.standard_normal((D, 1))),
        "w3": wdraw(),
        "b3": f32(0.5 / O * np.random.standard_normal((D, 1))),
        "offs": striped(np.random.permutation(np.tile(np.arange(S), 2))[:N]),
    }


def reference(table, x0, w0, b0, w1, b1, w2, b2, w3, b3, offs):
    idx = offs[:16].T.reshape(-1)
    rel = f64(table)[:, idx]
    x = np.tile(f64(x0), (1, B))
    x = layer(x, rel, f64(w0), f64(b0), f64(w1), f64(b1))
    return layer(x, rel, f64(w2), f64(b2), f64(w3), f64(b3))

@@ -1,0 +1,203 @@
+import concourse.mybir as mybir
+from concourse.masks import make_block_diagonal, make_identity
+
+F32 = mybir.dt.float32
+BF16 = mybir.dt.bfloat16
+U16 = mybir.dt.uint16
+MULT = mybir.AluOpType.mult
+ADD = mybir.AluOpType.add
+TANH = mybir.ActivationFunctionType.Tanh
+
+P = 128
+D = 512
+KB = D // P
+S = 4096
+B = 24
+O = 16
+T = B * O
+PAIRS = O * O
+N = B * PAIRS
+PIECE = 2048
+PIECES = N // PIECE
+PIECE_SCENES = PIECE // PAIRS
+PIECE_T = PIECE_SCENES * O
+
+FLOPS = 2 * (2 * D * N + 2 * D * D * B + 2 * D * D * T)
+
+
+def tile_gcn_b_kernel(tc, table, x0, w0, b0, w1, b1, w2, b2, w3, b3, offs, out):
+    nc = tc.nc
+    with (
+        tc.tile_pool(name="held", bufs=1) as held,
+        tc.tile_pool(name="x_pool", bufs=2) as x_pool,
+        tc.tile_pool(name="f32_products", bufs=3) as f32_products,
+        tc.tile_pool(name="bf16_products", bufs=2) as bf16_products,
+        tc.tile_pool(name="sums", bufs=2) as sums,
+        tc.psum_pool(name="setup_psum", bufs=1) as setup_psum,
+        tc.psum_pool(name="psum", bufs=2) as psum,
+    ):
+        offsets = held.tile([P, N // 16], U16, name="offsets")
+        nc.sync.dma_start(offsets[:], offs)
+
+        x_start = held.tile([P, KB, O], F32, name="x_start")
+        nc.scalar.dma_start(x_start[:], x0.rearrange("(k p) o -> p k o", p=P))
+
+        tables = []
+        for k in range(KB):
+            table_k = held.tile([P, S], F32, name=f"table{k}")
+            nc.sync.dma_start(table_k[:], table[k * P : (k + 1) * P, :])
+            tables.append(table_k)
+
+        wa_bf16, wb_f32 = [], []
+        for layer, (wa, wb) in enumerate(((w0, w1), (w2, w3))):
+            wa_tile = held.tile([P, KB, D], BF16, name=f"wa{layer}")
+            nc.sync.dma_start(wa_tile[:], wa.rearrange("(k p) m -> p k m", p=P))
+            wa_bf16.append(wa_tile)
+            wb_loaded = held.tile([P, KB, D], BF16, name="wb_loaded")
+            nc.sync.dma_start(wb_loaded[:], wb.rearrange("(k p) m -> p k m", p=P))
+            wb_tile = held.tile([P, KB, D], F32, name=f"wb{layer}")
+            nc.gpsimd.tensor_copy(wb_tile[:], wb_loaded[:])
+            wb_f32.append(wb_tile)
+
+        identity_f32 = held.tile([P, P], F32, name="identity_f32")
+        make_identity(nc, identity_f32[:])
+        identity_bf16 = held.tile([P, P], BF16, name="identity_bf16")
+        make_identity(nc, identity_bf16[:])
+        same_scene = held.tile([P, P], F32, name="same_scene")
+        make_block_diagonal(nc, same_scene[:], O)
+
+        bias_rows = held.tile([P, P], F32, name="bias_rows")
+        nc.gpsimd.memset(bias_rows[:], 0.0)
+        for i, b in enumerate((b0, b1, b2, b3)):
+            nc.scalar.dma_start(
+                bias_rows[i * KB : (i + 1) * KB, :], b.rearrange("(k p) one -> k (p one)", p=P)
+            )
+        bias_cols_psum = setup_psum.tile([P, P], F32, name="bias_cols_psum")
+        nc.tensor.transpose(bias_cols_psum[:], bias_rows[:], identity_f32[:])
+        bias_cols = held.tile([P, 4 * KB], F32, name="bias_cols")
+        nc.vector.tensor_copy(bias_cols[:], bias_cols_psum[:, 0 : 4 * KB])
+        layer_bias = []
+        for layer in range(2):
+            bias = held.tile([P, KB], F32, name=f"bias{layer}")
+            nc.vector.scalar_tensor_tensor(
+                bias[:],
+                bias_cols[:, (2 * layer + 1) * KB : (2 * layer + 2) * KB],
+                float(PAIRS // O),
+                bias_cols[:, 2 * layer * KB : (2 * layer + 1) * KB],
+                MULT,
+                ADD,
+            )
+            layer_bias.append(bias)
+
+        x0_of_entry = []
+        for k in range(KB):
+            x_k = held.tile([P, PIECE], F32, name=f"x0_of_entry{k}")
+            nc.gpsimd.tensor_copy(
+                x_k[:].rearrange("p (g o) -> p g o", o=O),
+                x_start[:, k, :].unsqueeze(1).to_broadcast([P, PIECE // O, O]),
+            )
+            x0_of_entry.append(x_k)
+        x0_bf16 = held.tile([P, KB, PIECE_T], BF16, name="x0_bf16")
+        nc.scalar.copy(
+            x0_bf16[:].rearrange("p k (b o) -> p k b o", o=O),
+            x_start[:].unsqueeze(2).to_broadcast([P, KB, PIECE_SCENES, O]),
+        )
+
+        x_of_entry = [x0_of_entry] * PIECES
+        x_bf16 = [x0_bf16] * PIECES
+        for layer in range(2):
+            next_of_entry, next_bf16 = [], []
+            for piece in range(PIECES):
+                piece_offsets = offsets[:, piece * PIECE // 16 : (piece + 1) * PIECE // 16]
+
+                msg_sum_t_psum = psum.tile([P, D], F32, name="msg_sum_t_psum")
+                for k in range(KB):
+                    p_f32 = f32_products.tile([P, PIECE], F32, name="p_f32")
+                    nc.vector.tensor_tensor(
+                        p_f32[:],
+                        tables[k][:].indirect(piece_offsets),
+                        x_of_entry[piece][k][:],
+                        MULT,
+                    )
+                    p_bf16 = bf16_products.tile([P, PIECE], BF16, name="p_bf16")
+                    nc.scalar.copy(p_bf16[:], p_f32[:])
+
+                    p_by_i = p_bf16[:].rearrange("p (b i o) -> p b i o", i=O, o=O)
+                    p_sum_psum = psum.tile([P, PIECE_T], F32, name="p_sum_psum")
+                    for i in range(O):
+                        nc.tensor.matmul(
+                            p_sum_psum[:].rearrange("p (b o) -> p b o", o=O),
+                            identity_bf16[:],
+                            p_by_i[:, :, i, :],
+                            start=(i == 0),
+                            stop=(i == O - 1),
+                        )
+                    p_sum = sums.tile([P, PIECE_T], F32, name="p_sum")
+                    nc.scalar.copy(p_sum[:], p_sum_psum[:])
+                    nc.tensor.matmul(
+                        msg_sum_t_psum[:],
+                        p_sum[:],
+                        wb_f32[layer][:, k, :],
+                        start=(k == 0),
+                        stop=(k == KB - 1),
+                    )
+                msg_sum_t = sums.tile([P, D], F32, name="msg_sum_t")
+                nc.scalar.mul(msg_sum_t[:], msg_sum_t_psum[:], 1.0 / O)
+
+                pre = psum.tile([P, KB, PIECE_T], F32, name="pre")
+                for m in range(KB):
+                    m_cols = slice(m * P, (m + 1) * P)
+                    for k in range(KB):
+                        nc.tensor.matmul(
+                            pre[:, m, :],
+                            wa_bf16[layer][:, k, m_cols],
+                            x_bf16[piece][:, k, :],
+                            start=(k == 0),
+                            stop=False,
+                        )
+                    x_m = x_of_entry[piece][m][:].rearrange("p (b i o) -> p b i o", i=O, o=O)
+                    nc.tensor.matmul(
+                        pre[:, m, :].rearrange("p (b o) -> p b o", o=O),
+                        identity_f32[:],
+                        x_m[:, :, 0, :],
+                        start=False,
+                        stop=False,
+                    )
+                    nc.tensor.matmul(
+                        pre[:, m, :], msg_sum_t[:, m_cols], same_scene[:], start=False, stop=True
+                    )
+
+                if layer == 0:
+                    x1_of_entry = []
+                    x1_bf16 = x_pool.tile([P, KB, PIECE_T], BF16, name="x1_bf16")
+                    for m in range(KB):
+                        x_m = x_pool.tile([P, PIECE], F32, name=f"x1_of_entry{m}")
+                        x_m_by_i = x_m[:].rearrange("p (b i o) -> p b i o", i=O, o=O)
+                        nc.scalar.activation(
+                            x_m_by_i,
+                            pre[:, m, :]
+                            .rearrange("p (b o) -> p b o", o=O)
+                            .unsqueeze(2)
+                            .to_broadcast([P, PIECE_SCENES, O, O]),
+                            TANH,
+                            bias=layer_bias[layer][:, m : m + 1],
+                        )
+                        nc.scalar.copy(
+                            x1_bf16[:, m, :].rearrange("p (b o) -> p b o", o=O), x_m_by_i[:, :, 0, :]
+                        )
+                        x1_of_entry.append(x_m)
+                    next_of_entry.append(x1_of_entry)
+                    next_bf16.append(x1_bf16)
+                else:
+                    x2 = sums.tile([P, KB, PIECE_T], F32, name="x2")
+                    for m in range(KB):
+                        nc.scalar.activation(
+                            x2[:, m, :], pre[:, m, :], TANH, bias=layer_bias[layer][:, m : m + 1]
+                        )
+                    nc.sync.dma_start(
+                        out.rearrange("(k p) t -> p k t", p=P)[
+                            :, :, piece * PIECE_T : (piece + 1) * PIECE_T
+                        ],
+                        x2[:],
+                    )
+            x_of_entry, x_bf16 = next_of_entry, next_bf16

@@ -33,31 +33,31 @@ def tile_gcn_b_kernel(tc, table, x0, w0, b0, w1, b1, w2, b2, w3, b3, offs, out):
         tc.tile_pool(name="f32_products", bufs=3) as f32_products,
         tc.tile_pool(name="bf16_products", bufs=2) as bf16_products,
         tc.tile_pool(name="sums", bufs=2) as sums,
-        tc.psum_pool(name="setup_psum", bufs=1) as setup_psum,
         tc.psum_pool(name="psum", bufs=2) as psum,
+        tc.psum_pool(name="pre_psum", bufs=1) as pre_psum,
     ):
-        offsets = held.tile([P, N // 16], U16, name="offsets")
-        nc.sync.dma_start(offsets[:], offs)
-
         x_start = held.tile([P, KB, O], F32, name="x_start")
         nc.scalar.dma_start(x_start[:], x0.rearrange("(k p) o -> p k o", p=P))
-
+        offsets = held.tile([P, N // 16], U16, name="offsets")
+        nc.sync.dma_start(offsets[:], offs)
+        bias_rows = held.tile([4 * KB, P], F32, name="bias_rows")
+        for i, b in enumerate((b0, b1, b2, b3)):
+            nc.scalar.dma_start(
+                bias_rows[i * KB : (i + 1) * KB, :], b.rearrange("(k p) one -> k (p one)", p=P)
+            )
         tables = []
         for k in range(KB):
             table_k = held.tile([P, S], F32, name=f"table{k}")
             nc.sync.dma_start(table_k[:], table[k * P : (k + 1) * P, :])
             tables.append(table_k)
-
-        wa_bf16, wb_f32 = [], []
+        wa_bf16, wb_bf16 = [], []
         for layer, (wa, wb) in enumerate(((w0, w1), (w2, w3))):
-            wa_tile = held.tile([P, KB, D], BF16, name=f"wa{layer}")
+            wb_tile = held.tile([P, KB, D], BF16, name=f"wb{layer}_bf16")
+            nc.sync.dma_start(wb_tile[:], wb.rearrange("(k p) m -> p k m", p=P))
+            wb_bf16.append(wb_tile)
+            wa_tile = held.tile([P, KB, D], BF16, name=f"wa{layer}_bf16")
             nc.sync.dma_start(wa_tile[:], wa.rearrange("(k p) m -> p k m", p=P))
             wa_bf16.append(wa_tile)
-            wb_loaded = held.tile([P, KB, D], BF16, name="wb_loaded")
-            nc.sync.dma_start(wb_loaded[:], wb.rearrange("(k p) m -> p k m", p=P))
-            wb_tile = held.tile([P, KB, D], F32, name=f"wb{layer}")
-            nc.gpsimd.tensor_copy(wb_tile[:], wb_loaded[:])
-            wb_f32.append(wb_tile)
 
         identity_f32 = held.tile([P, P], F32, name="identity_f32")
         make_identity(nc, identity_f32[:])
@@ -66,49 +66,63 @@ def tile_gcn_b_kernel(tc, table, x0, w0, b0, w1, b1, w2, b2, w3, b3, offs, out):
         same_scene = held.tile([P, P], F32, name="same_scene")
         make_block_diagonal(nc, same_scene[:], O)
 
-        bias_rows = held.tile([P, P], F32, name="bias_rows")
-        nc.gpsimd.memset(bias_rows[:], 0.0)
-        for i, b in enumerate((b0, b1, b2, b3)):
-            nc.scalar.dma_start(
-                bias_rows[i * KB : (i + 1) * KB, :], b.rearrange("(k p) one -> k (p one)", p=P)
-            )
-        bias_cols_psum = setup_psum.tile([P, P], F32, name="bias_cols_psum")
-        nc.tensor.transpose(bias_cols_psum[:], bias_rows[:], identity_f32[:])
-        bias_cols = held.tile([P, 4 * KB], F32, name="bias_cols")
-        nc.vector.tensor_copy(bias_cols[:], bias_cols_psum[:, 0 : 4 * KB])
-        layer_bias = []
-        for layer in range(2):
-            bias = held.tile([P, KB], F32, name=f"bias{layer}")
-            nc.vector.scalar_tensor_tensor(
-                bias[:],
-                bias_cols[:, (2 * layer + 1) * KB : (2 * layer + 2) * KB],
-                float(PAIRS // O),
-                bias_cols[:, 2 * layer * KB : (2 * layer + 1) * KB],
-                MULT,
-                ADD,
-            )
-            layer_bias.append(bias)
+        bias_cols_psum = psum.tile([P, 4 * KB], F32, name="bias_cols_psum", tag="p_sum_psum")
+        nc.tensor.matmul(
+            bias_cols_psum[:], bias_rows[:], identity_f32[0 : 4 * KB, 0 : 4 * KB], start=True, stop=True
+        )
+        bias_cols = held.tile([P, 2, 2, KB], F32, name="bias_cols")
+        nc.scalar.copy(bias_cols[:].rearrange("p l i k -> p (l i k)"), bias_cols_psum[:])
+        bb_sum = held.tile([P, 2, KB], F32, name="bb_sum")
+        nc.gpsimd.tensor_scalar(bb_sum[:], bias_cols[:, :, 1, :], float(PAIRS // O), None, MULT)
+        layer_bias = held.tile([P, 2, KB], F32, name="layer_bias")
+        nc.gpsimd.tensor_tensor(layer_bias[:], bb_sum[:], bias_cols[:, :, 0, :], ADD)
 
         x0_of_entry = []
         for k in range(KB):
-            x_k = held.tile([P, PIECE], F32, name=f"x0_of_entry{k}")
-            nc.gpsimd.tensor_copy(
+            x_k = x_pool.tile([P, PIECE], F32, name=f"x_of_entry{k}")
+            nc.scalar.copy(
                 x_k[:].rearrange("p (g o) -> p g o", o=O),
                 x_start[:, k, :].unsqueeze(1).to_broadcast([P, PIECE // O, O]),
             )
             x0_of_entry.append(x_k)
-        x0_bf16 = held.tile([P, KB, PIECE_T], BF16, name="x0_bf16")
+        x0_f32 = held.tile([P, KB, PIECE_T], F32, name="x0_f32")
         nc.scalar.copy(
-            x0_bf16[:].rearrange("p k (b o) -> p k b o", o=O),
+            x0_f32[:].rearrange("p k (b o) -> p k b o", o=O),
             x_start[:].unsqueeze(2).to_broadcast([P, KB, PIECE_SCENES, O]),
         )
+        x0_bf16 = held.tile([P, KB, PIECE_T], BF16, name="x0_bf16")
+        nc.scalar.copy(x0_bf16[:], x0_f32[:])
 
-        x_of_entry = [x0_of_entry] * PIECES
-        x_bf16 = [x0_bf16] * PIECES
+        wb_f32 = []
         for layer in range(2):
-            next_of_entry, next_bf16 = [], []
+            wb_tile = held.tile([P, KB, D], F32, name=f"wb{layer}_f32")
+            nc.scalar.copy(wb_tile[:], wb_bf16[layer][:])
+            wb_f32.append(wb_tile)
+
+        x_f32 = [x0_f32] * PIECES
+        x_bf16 = [x0_bf16] * PIECES
+        x_of_entry = {(0, piece, k): x0_of_entry[k] for piece in range(PIECES) for k in range(KB)}
+        to_repeat = []
+        for layer in range(2):
+            next_f32, next_bf16 = [], []
             for piece in range(PIECES):
                 piece_offsets = offsets[:, piece * PIECE // 16 : (piece + 1) * PIECE // 16]
+
+                pre = []
+                for m in range(KB):
+                    pre_m = pre_psum.tile([P, PIECE_T], F32, name=f"pre{m}")
+                    for k in range(KB):
+                        nc.tensor.matmul(
+                            pre_m[:],
+                            wa_bf16[layer][:, k, m * P : (m + 1) * P],
+                            x_bf16[piece][:, k, :],
+                            start=(k == 0),
+                            stop=False,
+                        )
+                    nc.tensor.matmul(
+                        pre_m[:], identity_f32[:], x_f32[piece][:, m, :], start=False, stop=False
+                    )
+                    pre.append(pre_m)
 
                 msg_sum_t_psum = psum.tile([P, D], F32, name="msg_sum_t_psum")
                 for k in range(KB):
@@ -116,11 +130,22 @@ def tile_gcn_b_kernel(tc, table, x0, w0, b0, w1, b1, w2, b2, w3, b3, offs, out):
                     nc.vector.tensor_tensor(
                         p_f32[:],
                         tables[k][:].indirect(piece_offsets),
-                        x_of_entry[piece][k][:],
+                        x_of_entry[layer, piece, k][:],
                         MULT,
                     )
                     p_bf16 = bf16_products.tile([P, PIECE], BF16, name="p_bf16")
                     nc.scalar.copy(p_bf16[:], p_f32[:])
+
+                    if to_repeat:
+                        later_piece, m, x_block = to_repeat.pop(0)
+                        x_m = x_pool.tile([P, PIECE], F32, name=f"x_of_entry{m}")
+                        nc.scalar.copy(
+                            x_m[:].rearrange("p (b i o) -> p b i o", i=O, o=O),
+                            x_block.rearrange("p (b o) -> p b o", o=O)
+                            .unsqueeze(2)
+                            .to_broadcast([P, PIECE_SCENES, O, O]),
+                        )
+                        x_of_entry[1, later_piece, m] = x_m
 
                     p_by_i = p_bf16[:].rearrange("p (b i o) -> p b i o", i=O, o=O)
                     p_sum_psum = psum.tile([P, PIECE_T], F32, name="p_sum_psum")
@@ -144,60 +169,27 @@ def tile_gcn_b_kernel(tc, table, x0, w0, b0, w1, b1, w2, b2, w3, b3, offs, out):
                 msg_sum_t = sums.tile([P, D], F32, name="msg_sum_t")
                 nc.scalar.mul(msg_sum_t[:], msg_sum_t_psum[:], 1.0 / O)
 
-                pre = psum.tile([P, KB, PIECE_T], F32, name="pre")
+                x_new = held.tile([P, KB, PIECE_T], F32, name=f"x{layer + 1}_f32_{piece}")
                 for m in range(KB):
-                    m_cols = slice(m * P, (m + 1) * P)
-                    for k in range(KB):
-                        nc.tensor.matmul(
-                            pre[:, m, :],
-                            wa_bf16[layer][:, k, m_cols],
-                            x_bf16[piece][:, k, :],
-                            start=(k == 0),
-                            stop=False,
-                        )
-                    x_m = x_of_entry[piece][m][:].rearrange("p (b i o) -> p b i o", i=O, o=O)
                     nc.tensor.matmul(
-                        pre[:, m, :].rearrange("p (b o) -> p b o", o=O),
-                        identity_f32[:],
-                        x_m[:, :, 0, :],
+                        pre[m][:],
+                        msg_sum_t[:, m * P : (m + 1) * P],
+                        same_scene[:],
                         start=False,
-                        stop=False,
+                        stop=True,
                     )
-                    nc.tensor.matmul(
-                        pre[:, m, :], msg_sum_t[:, m_cols], same_scene[:], start=False, stop=True
+                    nc.scalar.activation(
+                        x_new[:, m, :], pre[m][:], TANH, bias=layer_bias[:, layer, m : m + 1]
                     )
-
+                    if layer == 1:
+                        nc.sync.dma_start(
+                            out[m * P : (m + 1) * P, piece * PIECE_T : (piece + 1) * PIECE_T],
+                            x_new[:, m, :],
+                        )
                 if layer == 0:
-                    x1_of_entry = []
-                    x1_bf16 = x_pool.tile([P, KB, PIECE_T], BF16, name="x1_bf16")
-                    for m in range(KB):
-                        x_m = x_pool.tile([P, PIECE], F32, name=f"x1_of_entry{m}")
-                        x_m_by_i = x_m[:].rearrange("p (b i o) -> p b i o", i=O, o=O)
-                        nc.scalar.activation(
-                            x_m_by_i,
-                            pre[:, m, :]
-                            .rearrange("p (b o) -> p b o", o=O)
-                            .unsqueeze(2)
-                            .to_broadcast([P, PIECE_SCENES, O, O]),
-                            TANH,
-                            bias=layer_bias[layer][:, m : m + 1],
-                        )
-                        nc.scalar.copy(
-                            x1_bf16[:, m, :].rearrange("p (b o) -> p b o", o=O), x_m_by_i[:, :, 0, :]
-                        )
-                        x1_of_entry.append(x_m)
-                    next_of_entry.append(x1_of_entry)
-                    next_bf16.append(x1_bf16)
-                else:
-                    x2 = sums.tile([P, KB, PIECE_T], F32, name="x2")
-                    for m in range(KB):
-                        nc.scalar.activation(
-                            x2[:, m, :], pre[:, m, :], TANH, bias=layer_bias[layer][:, m : m + 1]
-                        )
-                    nc.sync.dma_start(
-                        out.rearrange("(k p) t -> p k t", p=P)[
-                            :, :, piece * PIECE_T : (piece + 1) * PIECE_T
-                        ],
-                        x2[:],
-                    )
-            x_of_entry, x_bf16 = next_of_entry, next_bf16
+                    x_new_bf16 = held.tile([P, KB, PIECE_T], BF16, name=f"x1_bf16_{piece}")
+                    nc.scalar.copy(x_new_bf16[:], x_new[:])
+                    next_f32.append(x_new)
+                    next_bf16.append(x_new_bf16)
+                    to_repeat.extend((piece, m, x_new[:, m, :]) for m in range(KB))
+            x_f32, x_bf16 = next_f32, next_bf16

@@ -34,7 +34,8 @@ def tile_gcn_b_kernel(tc, table, x0, w0, b0, w1, b1, w2, b2, w3, b3, offs, out):
         tc.tile_pool(name="bf16_products", bufs=2) as bf16_products,
         tc.tile_pool(name="sums", bufs=2) as sums,
         tc.psum_pool(name="psum", bufs=2) as psum,
-        tc.psum_pool(name="pre_psum", bufs=1) as pre_psum,
+        tc.psum_pool(name="msg_psum", bufs=1) as msg_psum,
+        tc.psum_pool(name="pre_psum", bufs=KB + 1) as pre_psum,
     ):
         x_start = held.tile([P, KB, O], F32, name="x_start")
         nc.scalar.dma_start(x_start[:], x0.rearrange("(k p) o -> p k o", p=P))
@@ -109,23 +110,22 @@ def tile_gcn_b_kernel(tc, table, x0, w0, b0, w1, b1, w2, b2, w3, b3, offs, out):
                 piece_offsets = offsets[:, piece * PIECE // 16 : (piece + 1) * PIECE // 16]
 
                 pre = []
-                for m in range(KB):
-                    pre_m = pre_psum.tile([P, PIECE_T], F32, name=f"pre{m}")
-                    for k in range(KB):
+                msg_sum_t_psum = msg_psum.tile([P, D], F32, name="msg_sum_t_psum")
+                for k in range(KB):
+                    pre_k = pre_psum.tile([P, PIECE_T], F32, name="pre")
+                    for k_in in range(KB):
                         nc.tensor.matmul(
-                            pre_m[:],
-                            wa_bf16[layer][:, k, m * P : (m + 1) * P],
-                            x_bf16[piece][:, k, :],
-                            start=(k == 0),
+                            pre_k[:],
+                            wa_bf16[layer][:, k_in, k * P : (k + 1) * P],
+                            x_bf16[piece][:, k_in, :],
+                            start=(k_in == 0),
                             stop=False,
                         )
                     nc.tensor.matmul(
-                        pre_m[:], identity_f32[:], x_f32[piece][:, m, :], start=False, stop=False
+                        pre_k[:], identity_f32[:], x_f32[piece][:, k, :], start=False, stop=False
                     )
-                    pre.append(pre_m)
+                    pre.append(pre_k)
 
-                msg_sum_t_psum = psum.tile([P, D], F32, name="msg_sum_t_psum")
-                for k in range(KB):
                     p_f32 = f32_products.tile([P, PIECE], F32, name="p_f32")
                     nc.vector.tensor_tensor(
                         p_f32[:],
@@ -139,12 +139,15 @@ def tile_gcn_b_kernel(tc, table, x0, w0, b0, w1, b1, w2, b2, w3, b3, offs, out):
                     if to_repeat:
                         later_piece, m, x_block = to_repeat.pop(0)
                         x_m = x_pool.tile([P, PIECE], F32, name=f"x_of_entry{m}")
+                        x_m_by_i = x_m[:].rearrange("p (b i o) -> p b i o", i=O, o=O)
                         nc.scalar.copy(
-                            x_m[:].rearrange("p (b i o) -> p b i o", i=O, o=O),
+                            x_m_by_i[:, :, 0:4, :],
                             x_block.rearrange("p (b o) -> p b o", o=O)
                             .unsqueeze(2)
-                            .to_broadcast([P, PIECE_SCENES, O, O]),
+                            .to_broadcast([P, PIECE_SCENES, 4, O]),
                         )
+                        nc.sync.dma_start(x_m_by_i[:, :, 4:8, :], x_m_by_i[:, :, 0:4, :])
+                        nc.sync.dma_start(x_m_by_i[:, :, 8:16, :], x_m_by_i[:, :, 0:8, :])
                         x_of_entry[1, later_piece, m] = x_m
 
                     p_by_i = p_bf16[:].rearrange("p (b i o) -> p b i o", i=O, o=O)

@@ -30,8 +30,8 @@ def tile_gcn_b_kernel(tc, table, x0, w0, b0, w1, b1, w2, b2, w3, b3, offs, out):
     with (
         tc.tile_pool(name="held", bufs=1) as held,
         tc.tile_pool(name="x_pool", bufs=2) as x_pool,
-        tc.tile_pool(name="f32_products", bufs=3) as f32_products,
-        tc.tile_pool(name="bf16_products", bufs=2) as bf16_products,
+        tc.tile_pool(name="f32_products", bufs=4) as f32_products,
+        tc.tile_pool(name="bf16_products", bufs=3) as bf16_products,
         tc.tile_pool(name="sums", bufs=2) as sums,
         tc.psum_pool(name="psum", bufs=2) as psum,
         tc.psum_pool(name="msg_psum", bufs=1) as msg_psum,

@@ -21,6 +21,7 @@ PIECE = 2048
 PIECES = N // PIECE
 PIECE_SCENES = PIECE // PAIRS
 PIECE_T = PIECE_SCENES * O
+SCALAR_COPIES = 4
 
 FLOPS = 2 * (2 * D * N + 2 * D * D * B + 2 * D * D * T)
 
@@ -30,8 +31,8 @@ def tile_gcn_b_kernel(tc, table, x0, w0, b0, w1, b1, w2, b2, w3, b3, offs, out):
     with (
         tc.tile_pool(name="held", bufs=1) as held,
         tc.tile_pool(name="x_pool", bufs=2) as x_pool,
-        tc.tile_pool(name="f32_products", bufs=4) as f32_products,
-        tc.tile_pool(name="bf16_products", bufs=3) as bf16_products,
+        tc.tile_pool(name="f32_products", bufs=3) as f32_products,
+        tc.tile_pool(name="bf16_products", bufs=2) as bf16_products,
         tc.tile_pool(name="sums", bufs=2) as sums,
         tc.psum_pool(name="psum", bufs=2) as psum,
         tc.psum_pool(name="msg_psum", bufs=1) as msg_psum,
@@ -67,16 +68,15 @@ def tile_gcn_b_kernel(tc, table, x0, w0, b0, w1, b1, w2, b2, w3, b3, offs, out):
         same_scene = held.tile([P, P], F32, name="same_scene")
         make_block_diagonal(nc, same_scene[:], O)
 
-        bias_cols_psum = psum.tile([P, 4 * KB], F32, name="bias_cols_psum", tag="p_sum_psum")
-        nc.tensor.matmul(
-            bias_cols_psum[:], bias_rows[:], identity_f32[0 : 4 * KB, 0 : 4 * KB], start=True, stop=True
-        )
-        bias_cols = held.tile([P, 2, 2, KB], F32, name="bias_cols")
-        nc.scalar.copy(bias_cols[:].rearrange("p l i k -> p (l i k)"), bias_cols_psum[:])
-        bb_sum = held.tile([P, 2, KB], F32, name="bb_sum")
-        nc.gpsimd.tensor_scalar(bb_sum[:], bias_cols[:, :, 1, :], float(PAIRS // O), None, MULT)
+        row_is = identity_f32[0 : 4 * KB, 0 : 4 * KB].rearrange("r (l i k) -> r l i k", l=2, i=2)
+        bb_weight = held.tile([4 * KB, 2, KB], F32, name="bb_weight")
+        nc.gpsimd.tensor_scalar(bb_weight[:], row_is[:, :, 1, :], float(PAIRS // O), None, MULT)
+        combine = held.tile([4 * KB, 2, KB], F32, name="combine")
+        nc.gpsimd.tensor_tensor(combine[:], bb_weight[:], row_is[:, :, 0, :], ADD)
+        layer_bias_psum = psum.tile([P, 2, KB], F32, name="layer_bias_psum", tag="p_sum_psum")
+        nc.tensor.matmul(layer_bias_psum[:], bias_rows[:], combine[:], start=True, stop=True)
         layer_bias = held.tile([P, 2, KB], F32, name="layer_bias")
-        nc.gpsimd.tensor_tensor(layer_bias[:], bb_sum[:], bias_cols[:, :, 0, :], ADD)
+        nc.scalar.copy(layer_bias[:], layer_bias_psum[:])
 
         x0_of_entry = []
         for k in range(KB):
@@ -103,7 +103,7 @@ def tile_gcn_b_kernel(tc, table, x0, w0, b0, w1, b1, w2, b2, w3, b3, offs, out):
         x_f32 = [x0_f32] * PIECES
         x_bf16 = [x0_bf16] * PIECES
         x_of_entry = {(0, piece, k): x0_of_entry[k] for piece in range(PIECES) for k in range(KB)}
-        to_repeat = []
+        x1_to_repeat = None
         for layer in range(2):
             next_f32, next_bf16 = [], []
             for piece in range(PIECES):
@@ -112,19 +112,20 @@ def tile_gcn_b_kernel(tc, table, x0, w0, b0, w1, b1, w2, b2, w3, b3, offs, out):
                 pre = []
                 msg_sum_t_psum = msg_psum.tile([P, D], F32, name="msg_sum_t_psum")
                 for k in range(KB):
-                    pre_k = pre_psum.tile([P, PIECE_T], F32, name="pre")
+                    m = k
+                    pre_m = pre_psum.tile([P, PIECE_T], F32, name="pre")
                     for k_in in range(KB):
                         nc.tensor.matmul(
-                            pre_k[:],
-                            wa_bf16[layer][:, k_in, k * P : (k + 1) * P],
+                            pre_m[:],
+                            wa_bf16[layer][:, k_in, m * P : (m + 1) * P],
                             x_bf16[piece][:, k_in, :],
                             start=(k_in == 0),
                             stop=False,
                         )
                     nc.tensor.matmul(
-                        pre_k[:], identity_f32[:], x_f32[piece][:, k, :], start=False, stop=False
+                        pre_m[:], identity_f32[:], x_f32[piece][:, m, :], start=False, stop=False
                     )
-                    pre.append(pre_k)
+                    pre.append(pre_m)
 
                     p_f32 = f32_products.tile([P, PIECE], F32, name="p_f32")
                     nc.vector.tensor_tensor(
@@ -136,19 +137,26 @@ def tile_gcn_b_kernel(tc, table, x0, w0, b0, w1, b1, w2, b2, w3, b3, offs, out):
                     p_bf16 = bf16_products.tile([P, PIECE], BF16, name="p_bf16")
                     nc.scalar.copy(p_bf16[:], p_f32[:])
 
-                    if to_repeat:
-                        later_piece, m, x_block = to_repeat.pop(0)
-                        x_m = x_pool.tile([P, PIECE], F32, name=f"x_of_entry{m}")
-                        x_m_by_i = x_m[:].rearrange("p (b i o) -> p b i o", i=O, o=O)
+                    if x1_to_repeat:
+                        x1_piece, x1 = x1_to_repeat
+                        x_k = x_pool.tile([P, PIECE], F32, name=f"x_of_entry{k}")
+                        x_k_by_i = x_k[:].rearrange("p (b i o) -> p b i o", i=O, o=O)
                         nc.scalar.copy(
-                            x_m_by_i[:, :, 0:4, :],
-                            x_block.rearrange("p (b o) -> p b o", o=O)
+                            x_k_by_i[:, :, 0:SCALAR_COPIES, :],
+                            x1[:, k, :]
+                            .rearrange("p (b o) -> p b o", o=O)
                             .unsqueeze(2)
-                            .to_broadcast([P, PIECE_SCENES, 4, O]),
+                            .to_broadcast([P, PIECE_SCENES, SCALAR_COPIES, O]),
                         )
-                        nc.sync.dma_start(x_m_by_i[:, :, 4:8, :], x_m_by_i[:, :, 0:4, :])
-                        nc.sync.dma_start(x_m_by_i[:, :, 8:16, :], x_m_by_i[:, :, 0:8, :])
-                        x_of_entry[1, later_piece, m] = x_m
+                        nc.sync.dma_start(
+                            x_k_by_i[:, :, SCALAR_COPIES : 2 * SCALAR_COPIES, :],
+                            x_k_by_i[:, :, 0:SCALAR_COPIES, :],
+                        )
+                        nc.sync.dma_start(
+                            x_k_by_i[:, :, 2 * SCALAR_COPIES : O, :],
+                            x_k_by_i[:, :, 0 : 2 * SCALAR_COPIES, :],
+                        )
+                        x_of_entry[1, x1_piece, k] = x_k
 
                     p_by_i = p_bf16[:].rearrange("p (b i o) -> p b i o", i=O, o=O)
                     p_sum_psum = psum.tile([P, PIECE_T], F32, name="p_sum_psum")
@@ -194,5 +202,5 @@ def tile_gcn_b_kernel(tc, table, x0, w0, b0, w1, b1, w2, b2, w3, b3, offs, out):
                     nc.scalar.copy(x_new_bf16[:], x_new[:])
                     next_f32.append(x_new)
                     next_bf16.append(x_new_bf16)
-                    to_repeat.extend((piece, m, x_new[:, m, :]) for m in range(KB))
+                x1_to_repeat = (piece, x_new) if layer == 0 else None
             x_f32, x_bf16 = next_f32, next_bf16

@@ -1,5 +1,5 @@
 import concourse.mybir as mybir
-from concourse.masks import make_block_diagonal, make_identity
+from concourse.masks import make_identity
 
 F32 = mybir.dt.float32
 BF16 = mybir.dt.bfloat16
@@ -7,6 +7,7 @@ U16 = mybir.dt.uint16
 MULT = mybir.AluOpType.mult
 ADD = mybir.AluOpType.add
 TANH = mybir.ActivationFunctionType.Tanh
+COPY = mybir.ActivationFunctionType.Copy
 
 P = 128
 D = 512
@@ -31,12 +32,9 @@ def tile_gcn_b_kernel(tc, table, x0, w0, b0, w1, b1, w2, b2, w3, b3, offs, out):
     with (
         tc.tile_pool(name="held", bufs=1) as held,
         tc.tile_pool(name="x_pool", bufs=2) as x_pool,
-        tc.tile_pool(name="f32_products", bufs=3) as f32_products,
-        tc.tile_pool(name="bf16_products", bufs=2) as bf16_products,
+        tc.tile_pool(name="products", bufs=3) as products,
         tc.tile_pool(name="sums", bufs=2) as sums,
-        tc.psum_pool(name="psum", bufs=2) as psum,
-        tc.psum_pool(name="msg_psum", bufs=1) as msg_psum,
-        tc.psum_pool(name="pre_psum", bufs=KB + 1) as pre_psum,
+        tc.psum_pool(name="pre_psum", bufs=2 * KB) as pre_psum,
     ):
         x_start = held.tile([P, KB, O], F32, name="x_start")
         nc.scalar.dma_start(x_start[:], x0.rearrange("(k p) o -> p k o", p=P))
@@ -63,17 +61,13 @@ def tile_gcn_b_kernel(tc, table, x0, w0, b0, w1, b1, w2, b2, w3, b3, offs, out):
 
         identity_f32 = held.tile([P, P], F32, name="identity_f32")
         make_identity(nc, identity_f32[:])
-        identity_bf16 = held.tile([P, P], BF16, name="identity_bf16")
-        make_identity(nc, identity_bf16[:])
-        same_scene = held.tile([P, P], F32, name="same_scene")
-        make_block_diagonal(nc, same_scene[:], O)
 
         row_is = identity_f32[0 : 4 * KB, 0 : 4 * KB].rearrange("r (l i k) -> r l i k", l=2, i=2)
         bb_weight = held.tile([4 * KB, 2, KB], F32, name="bb_weight")
         nc.gpsimd.tensor_scalar(bb_weight[:], row_is[:, :, 1, :], float(PAIRS // O), None, MULT)
         combine = held.tile([4 * KB, 2, KB], F32, name="combine")
         nc.gpsimd.tensor_tensor(combine[:], bb_weight[:], row_is[:, :, 0, :], ADD)
-        layer_bias_psum = psum.tile([P, 2, KB], F32, name="layer_bias_psum", tag="p_sum_psum")
+        layer_bias_psum = pre_psum.tile([P, 2, KB], F32, name="layer_bias_psum", tag="pre")
         nc.tensor.matmul(layer_bias_psum[:], bias_rows[:], combine[:], start=True, stop=True)
         layer_bias = held.tile([P, 2, KB], F32, name="layer_bias")
         nc.scalar.copy(layer_bias[:], layer_bias_psum[:])
@@ -110,9 +104,7 @@ def tile_gcn_b_kernel(tc, table, x0, w0, b0, w1, b1, w2, b2, w3, b3, offs, out):
                 piece_offsets = offsets[:, piece * PIECE // 16 : (piece + 1) * PIECE // 16]
 
                 pre = []
-                msg_sum_t_psum = msg_psum.tile([P, D], F32, name="msg_sum_t_psum")
-                for k in range(KB):
-                    m = k
+                for m in range(KB):
                     pre_m = pre_psum.tile([P, PIECE_T], F32, name="pre")
                     for k_in in range(KB):
                         nc.tensor.matmul(
@@ -127,15 +119,24 @@ def tile_gcn_b_kernel(tc, table, x0, w0, b0, w1, b1, w2, b2, w3, b3, offs, out):
                     )
                     pre.append(pre_m)
 
-                    p_f32 = f32_products.tile([P, PIECE], F32, name="p_f32")
+                for k in range(KB):
+                    p_f32 = products.tile([P, PIECE], F32, name="p_f32")
                     nc.vector.tensor_tensor(
                         p_f32[:],
                         tables[k][:].indirect(piece_offsets),
                         x_of_entry[layer, piece, k][:],
                         MULT,
                     )
-                    p_bf16 = bf16_products.tile([P, PIECE], BF16, name="p_bf16")
-                    nc.scalar.copy(p_bf16[:], p_f32[:])
+                    p_mean = sums.tile([P, PIECE_SCENES], F32, name="p_mean")
+                    for b in range(PIECE_SCENES):
+                        unused_copy = sums.tile([P, PAIRS], BF16, name="unused_copy")
+                        nc.scalar.activation(
+                            unused_copy[:],
+                            p_f32[:, b * PAIRS : (b + 1) * PAIRS],
+                            COPY,
+                            scale=1.0 / O,
+                            accum_out=p_mean[:, b : b + 1],
+                        )
 
                     if x1_to_repeat:
                         x1_piece, x1 = x1_to_repeat
@@ -158,37 +159,17 @@ def tile_gcn_b_kernel(tc, table, x0, w0, b0, w1, b1, w2, b2, w3, b3, offs, out):
                         )
                         x_of_entry[1, x1_piece, k] = x_k
 
-                    p_by_i = p_bf16[:].rearrange("p (b i o) -> p b i o", i=O, o=O)
-                    p_sum_psum = psum.tile([P, PIECE_T], F32, name="p_sum_psum")
-                    for i in range(O):
+                    for m in range(KB):
                         nc.tensor.matmul(
-                            p_sum_psum[:].rearrange("p (b o) -> p b o", o=O),
-                            identity_bf16[:],
-                            p_by_i[:, :, i, :],
-                            start=(i == 0),
-                            stop=(i == O - 1),
+                            pre[m][:].rearrange("p (b o) -> p b o", o=O),
+                            wb_f32[layer][:, k, m * P : (m + 1) * P],
+                            p_mean[:].unsqueeze(2).to_broadcast([P, PIECE_SCENES, O]),
+                            start=False,
+                            stop=(k == KB - 1),
                         )
-                    p_sum = sums.tile([P, PIECE_T], F32, name="p_sum")
-                    nc.scalar.copy(p_sum[:], p_sum_psum[:])
-                    nc.tensor.matmul(
-                        msg_sum_t_psum[:],
-                        p_sum[:],
-                        wb_f32[layer][:, k, :],
-                        start=(k == 0),
-                        stop=(k == KB - 1),
-                    )
-                msg_sum_t = sums.tile([P, D], F32, name="msg_sum_t")
-                nc.scalar.mul(msg_sum_t[:], msg_sum_t_psum[:], 1.0 / O)
 
                 x_new = held.tile([P, KB, PIECE_T], F32, name=f"x{layer + 1}_f32_{piece}")
                 for m in range(KB):
-                    nc.tensor.matmul(
-                        pre[m][:],
-                        msg_sum_t[:, m * P : (m + 1) * P],
-                        same_scene[:],
-                        start=False,
-                        stop=True,
-                    )
                     nc.scalar.activation(
                         x_new[:, m, :], pre[m][:], TANH, bias=layer_bias[:, layer, m : m + 1]
                     )

@@ -27,13 +27,23 @@ SCALAR_COPIES = 4
 FLOPS = 2 * (2 * D * N + 2 * D * D * B + 2 * D * D * T)
 
 
+def halving_cuts(scenes):
+    cuts, first = [], 0
+    while scenes - first > 1:
+        cuts.append((first, (scenes - first) // 2))
+        first += (scenes - first) // 2
+    cuts.append((first, scenes - first))
+    return cuts
+
+
 def tile_gcn_b_kernel(tc, table, x0, w0, b0, w1, b1, w2, b2, w3, b3, offs, out):
     nc = tc.nc
     with (
         tc.tile_pool(name="held", bufs=1) as held,
         tc.tile_pool(name="x_pool", bufs=2) as x_pool,
-        tc.tile_pool(name="products", bufs=3) as products,
-        tc.tile_pool(name="sums", bufs=2) as sums,
+        tc.tile_pool(name="products", bufs=4) as products,
+        tc.tile_pool(name="unused", bufs=2) as unused,
+        tc.tile_pool(name="sums", bufs=2 * KB) as sums,
         tc.psum_pool(name="pre_psum", bufs=2 * KB) as pre_psum,
     ):
         x_start = held.tile([P, KB, O], F32, name="x_start")
@@ -101,8 +111,6 @@ def tile_gcn_b_kernel(tc, table, x0, w0, b0, w1, b1, w2, b2, w3, b3, offs, out):
         for layer in range(2):
             next_f32, next_bf16 = [], []
             for piece in range(PIECES):
-                piece_offsets = offsets[:, piece * PIECE // 16 : (piece + 1) * PIECE // 16]
-
                 pre = []
                 for m in range(KB):
                     pre_m = pre_psum.tile([P, PIECE_T], F32, name="pre")
@@ -120,22 +128,38 @@ def tile_gcn_b_kernel(tc, table, x0, w0, b0, w1, b1, w2, b2, w3, b3, offs, out):
                     pre.append(pre_m)
 
                 for k in range(KB):
-                    p_f32 = products.tile([P, PIECE], F32, name="p_f32")
-                    nc.vector.tensor_tensor(
-                        p_f32[:],
-                        tables[k][:].indirect(piece_offsets),
-                        x_of_entry[layer, piece, k][:],
-                        MULT,
-                    )
+                    is_last_lookup = layer == 1 and piece == PIECES - 1 and k == KB - 1
+                    cuts = halving_cuts(PIECE_SCENES) if is_last_lookup else [(0, PIECE_SCENES)]
                     p_mean = sums.tile([P, PIECE_SCENES], F32, name="p_mean")
-                    for b in range(PIECE_SCENES):
-                        unused_copy = sums.tile([P, PAIRS], BF16, name="unused_copy")
-                        nc.scalar.activation(
-                            unused_copy[:],
-                            p_f32[:, b * PAIRS : (b + 1) * PAIRS],
-                            COPY,
-                            scale=1.0 / O,
-                            accum_out=p_mean[:, b : b + 1],
+                    for first_scene, scenes in cuts:
+                        first_column = (piece * PIECE_SCENES + first_scene) * PAIRS // 16
+                        p_f32 = products.tile([P, scenes * PAIRS], F32, name="p_f32")
+                        nc.vector.tensor_tensor(
+                            p_f32[:],
+                            tables[k][:].indirect(
+                                offsets[:, first_column : first_column + scenes * PAIRS // 16]
+                            ),
+                            x_of_entry[layer, piece, k][
+                                :, first_scene * PAIRS : (first_scene + scenes) * PAIRS
+                            ],
+                            MULT,
+                        )
+                        for b in range(scenes):
+                            unused_copy = unused.tile([P, PAIRS], BF16, name="unused_copy")
+                            nc.scalar.activation(
+                                unused_copy[:],
+                                p_f32[:, b * PAIRS : (b + 1) * PAIRS],
+                                COPY,
+                                scale=1.0 / O,
+                                accum_out=p_mean[:, first_scene + b : first_scene + b + 1],
+                            )
+                    for m in range(KB):
+                        nc.tensor.matmul(
+                            pre[m][:].rearrange("p (b o) -> p b o", o=O),
+                            wb_f32[layer][:, k, m * P : (m + 1) * P],
+                            p_mean[:].unsqueeze(2).to_broadcast([P, PIECE_SCENES, O]),
+                            start=False,
+                            stop=(k == KB - 1),
                         )
 
                     if x1_to_repeat:
@@ -158,15 +182,6 @@ def tile_gcn_b_kernel(tc, table, x0, w0, b0, w1, b1, w2, b2, w3, b3, offs, out):
                             x_k_by_i[:, :, 0 : 2 * SCALAR_COPIES, :],
                         )
                         x_of_entry[1, x1_piece, k] = x_k
-
-                    for m in range(KB):
-                        nc.tensor.matmul(
-                            pre[m][:].rearrange("p (b o) -> p b o", o=O),
-                            wb_f32[layer][:, k, m * P : (m + 1) * P],
-                            p_mean[:].unsqueeze(2).to_broadcast([P, PIECE_SCENES, O]),
-                            start=False,
-                            stop=(k == KB - 1),
-                        )
 
                 x_new = held.tile([P, KB, PIECE_T], F32, name=f"x{layer + 1}_f32_{piece}")
                 for m in range(KB):

@@ -98,12 +98,6 @@ def tile_gcn_b_kernel(tc, table, x0, w0, b0, w1, b1, w2, b2, w3, b3, offs, out):
         x0_bf16 = held.tile([P, KB, PIECE_T], BF16, name="x0_bf16")
         nc.scalar.copy(x0_bf16[:], x0_f32[:])
 
-        wb_f32 = []
-        for layer in range(2):
-            wb_tile = held.tile([P, KB, D], F32, name=f"wb{layer}_f32")
-            nc.scalar.copy(wb_tile[:], wb_bf16[layer][:])
-            wb_f32.append(wb_tile)
-
         x_f32 = [x0_f32] * PIECES
         x_bf16 = [x0_bf16] * PIECES
         x_of_entry = {(0, piece, k): x0_of_entry[k] for piece in range(PIECES) for k in range(KB)}
@@ -130,7 +124,7 @@ def tile_gcn_b_kernel(tc, table, x0, w0, b0, w1, b1, w2, b2, w3, b3, offs, out):
                 for k in range(KB):
                     is_last_lookup = layer == 1 and piece == PIECES - 1 and k == KB - 1
                     cuts = halving_cuts(PIECE_SCENES) if is_last_lookup else [(0, PIECE_SCENES)]
-                    p_mean = sums.tile([P, PIECE_SCENES], F32, name="p_mean")
+                    p_mean = sums.tile([P, PIECE_SCENES], BF16, name="p_mean")
                     for first_scene, scenes in cuts:
                         first_column = (piece * PIECE_SCENES + first_scene) * PAIRS // 16
                         p_f32 = products.tile([P, scenes * PAIRS], F32, name="p_f32")
@@ -146,17 +140,18 @@ def tile_gcn_b_kernel(tc, table, x0, w0, b0, w1, b1, w2, b2, w3, b3, offs, out):
                         )
                         for b in range(scenes):
                             unused_copy = unused.tile([P, PAIRS], BF16, name="unused_copy")
-                            nc.scalar.activation(
-                                unused_copy[:],
-                                p_f32[:, b * PAIRS : (b + 1) * PAIRS],
-                                COPY,
-                                scale=1.0 / O,
-                                accum_out=p_mean[:, first_scene + b : first_scene + b + 1],
-                            )
+                            with nc.allow_low_precision(reason="the sum is a bfloat16 matmul's operand"):
+                                nc.scalar.activation(
+                                    unused_copy[:],
+                                    p_f32[:, b * PAIRS : (b + 1) * PAIRS],
+                                    COPY,
+                                    scale=1.0 / O,
+                                    accum_out=p_mean[:, first_scene + b : first_scene + b + 1],
+                                )
                     for m in range(KB):
                         nc.tensor.matmul(
                             pre[m][:].rearrange("p (b o) -> p b o", o=O),
-                            wb_f32[layer][:, k, m * P : (m + 1) * P],
+                            wb_bf16[layer][:, k, m * P : (m + 1) * P],
                             p_mean[:].unsqueeze(2).to_broadcast([P, PIECE_SCENES, O]),
                             start=False,
                             stop=(k == KB - 1),

@@ -18,22 +18,19 @@ O = 16
 T = B * O
 PAIRS = O * O
 N = B * PAIRS
-PIECE = 2048
-PIECES = N // PIECE
-PIECE_SCENES = PIECE // PAIRS
-PIECE_T = PIECE_SCENES * O
+LOOKUP = 8
+PART = 8
+TAIL = 2
 SCALAR_COPIES = 4
+
+assert LOOKUP % PART == 0 and KB * PART * O <= 512 and TAIL < PART
 
 FLOPS = 2 * (2 * D * N + 2 * D * D * B + 2 * D * D * T)
 
 
-def halving_cuts(scenes):
-    cuts, first = [], 0
-    while scenes - first > 1:
-        cuts.append((first, (scenes - first) // 2))
-        first += (scenes - first) // 2
-    cuts.append((first, scenes - first))
-    return cuts
+def cut(first, last, size):
+    starts = [b for b in range(first, last) if b == first or b % size == 0]
+    return [(b, end - b) for b, end in zip(starts, starts[1:] + [last])]
 
 
 def tile_gcn_b_kernel(tc, table, x0, w0, b0, w1, b1, w2, b2, w3, b3, offs, out):
@@ -44,7 +41,7 @@ def tile_gcn_b_kernel(tc, table, x0, w0, b0, w1, b1, w2, b2, w3, b3, offs, out):
         tc.tile_pool(name="products", bufs=4) as products,
         tc.tile_pool(name="unused", bufs=2) as unused,
         tc.tile_pool(name="sums", bufs=2 * KB) as sums,
-        tc.psum_pool(name="pre_psum", bufs=2 * KB) as pre_psum,
+        tc.psum_pool(name="pre_psum", bufs=2) as pre_psum,
     ):
         x_start = held.tile([P, KB, O], F32, name="x_start")
         nc.scalar.dma_start(x_start[:], x0.rearrange("(k p) o -> p k o", p=P))
@@ -77,68 +74,78 @@ def tile_gcn_b_kernel(tc, table, x0, w0, b0, w1, b1, w2, b2, w3, b3, offs, out):
         nc.gpsimd.tensor_scalar(bb_weight[:], row_is[:, :, 1, :], float(PAIRS // O), None, MULT)
         combine = held.tile([4 * KB, 2, KB], F32, name="combine")
         nc.gpsimd.tensor_tensor(combine[:], bb_weight[:], row_is[:, :, 0, :], ADD)
-        layer_bias_psum = pre_psum.tile([P, 2, KB], F32, name="layer_bias_psum", tag="pre")
-        nc.tensor.matmul(layer_bias_psum[:], bias_rows[:], combine[:], start=True, stop=True)
-        layer_bias = held.tile([P, 2, KB], F32, name="layer_bias")
-        nc.scalar.copy(layer_bias[:], layer_bias_psum[:])
 
-        x0_of_entry = []
+        x_of_entry = {}
         for k in range(KB):
-            x_k = x_pool.tile([P, PIECE], F32, name=f"x_of_entry{k}")
+            x_k = x_pool.tile([P, LOOKUP * PAIRS], F32, name=f"x_of_entry{k}")
             nc.scalar.copy(
                 x_k[:].rearrange("p (g o) -> p g o", o=O),
-                x_start[:, k, :].unsqueeze(1).to_broadcast([P, PIECE // O, O]),
+                x_start[:, k, :].unsqueeze(1).to_broadcast([P, LOOKUP * O, O]),
             )
-            x0_of_entry.append(x_k)
-        x0_f32 = held.tile([P, KB, PIECE_T], F32, name="x0_f32")
+            for i in range(B // LOOKUP):
+                x_of_entry[0, i, k] = x_k
+        x0_f32 = held.tile([P, KB, PART * O], F32, name="x0_f32")
         nc.scalar.copy(
             x0_f32[:].rearrange("p k (b o) -> p k b o", o=O),
-            x_start[:].unsqueeze(2).to_broadcast([P, KB, PIECE_SCENES, O]),
+            x_start[:].unsqueeze(2).to_broadcast([P, KB, PART, O]),
         )
-        x0_bf16 = held.tile([P, KB, PIECE_T], BF16, name="x0_bf16")
+        x0_bf16 = held.tile([P, KB, PART * O], BF16, name="x0_bf16")
         nc.scalar.copy(x0_bf16[:], x0_f32[:])
 
-        x_f32 = [x0_f32] * PIECES
-        x_bf16 = [x0_bf16] * PIECES
-        x_of_entry = {(0, piece, k): x0_of_entry[k] for piece in range(PIECES) for k in range(KB)}
-        x1_to_repeat = None
+        x_f32 = [x0_f32] * (B // PART)
+        x_bf16 = [x0_bf16] * (B // PART)
+        to_repeat = []
         for layer in range(2):
+            pieces = cut(0, B, LOOKUP)
+            if layer == 1:
+                pieces[-1:] = [(B - LOOKUP, LOOKUP - TAIL), (B - TAIL, TAIL)]
             next_f32, next_bf16 = [], []
-            for piece in range(PIECES):
-                pre = []
-                for m in range(KB):
-                    pre_m = pre_psum.tile([P, PIECE_T], F32, name="pre")
-                    for k_in in range(KB):
-                        nc.tensor.matmul(
-                            pre_m[:],
-                            wa_bf16[layer][:, k_in, m * P : (m + 1) * P],
-                            x_bf16[piece][:, k_in, :],
-                            start=(k_in == 0),
-                            stop=False,
-                        )
+            for first, scenes in pieces:
+                parts = []
+                for part_first, part_scenes in cut(first, first + scenes, PART):
+                    columns = part_scenes * O
+                    x_columns = slice(part_first % PART * O, part_first % PART * O + columns)
+                    pre = pre_psum.tile([P, KB, columns], F32, name="pre")
                     nc.tensor.matmul(
-                        pre_m[:], identity_f32[:], x_f32[piece][:, m, :], start=False, stop=False
+                        pre[:],
+                        identity_f32[:],
+                        x_f32[part_first // PART][:, :, x_columns],
+                        start=True,
+                        stop=False,
                     )
-                    pre.append(pre_m)
+                    nc.tensor.matmul(
+                        pre[:],
+                        bias_rows[:],
+                        combine[:, layer, :].unsqueeze(2).to_broadcast([4 * KB, KB, columns]),
+                        start=False,
+                        stop=False,
+                    )
+                    for m in range(KB):
+                        for k_in in range(KB):
+                            nc.tensor.matmul(
+                                pre[:, m, :],
+                                wa_bf16[layer][:, k_in, m * P : (m + 1) * P],
+                                x_bf16[part_first // PART][:, k_in, x_columns],
+                                start=False,
+                                stop=False,
+                            )
+                    parts.append((part_first, part_scenes, pre))
 
                 for k in range(KB):
-                    is_last_lookup = layer == 1 and piece == PIECES - 1 and k == KB - 1
-                    cuts = halving_cuts(PIECE_SCENES) if is_last_lookup else [(0, PIECE_SCENES)]
-                    p_mean = sums.tile([P, PIECE_SCENES], BF16, name="p_mean")
-                    for first_scene, scenes in cuts:
-                        first_column = (piece * PIECE_SCENES + first_scene) * PAIRS // 16
-                        p_f32 = products.tile([P, scenes * PAIRS], F32, name="p_f32")
+                    is_last = layer == 1 and first == B - TAIL and k == KB - 1
+                    p_mean = sums.tile([P, scenes], BF16, name="p_mean")
+                    for cut_first, cut_scenes in cut(first, first + scenes, 1 if is_last else LOOKUP):
+                        x_first = cut_first % LOOKUP * PAIRS
+                        p_f32 = products.tile([P, cut_scenes * PAIRS], F32, name="p_f32")
                         nc.vector.tensor_tensor(
                             p_f32[:],
                             tables[k][:].indirect(
-                                offsets[:, first_column : first_column + scenes * PAIRS // 16]
+                                offsets[:, cut_first * PAIRS // 16 : (cut_first + cut_scenes) * PAIRS // 16]
                             ),
-                            x_of_entry[layer, piece, k][
-                                :, first_scene * PAIRS : (first_scene + scenes) * PAIRS
-                            ],
+                            x_of_entry[layer, first // LOOKUP, k][:, x_first : x_first + cut_scenes * PAIRS],
                             MULT,
                         )
-                        for b in range(scenes):
+                        for b in range(cut_scenes):
                             unused_copy = unused.tile([P, PAIRS], BF16, name="unused_copy")
                             with nc.allow_low_precision(reason="the sum is a bfloat16 matmul's operand"):
                                 nc.scalar.activation(
@@ -146,28 +153,32 @@ def tile_gcn_b_kernel(tc, table, x0, w0, b0, w1, b1, w2, b2, w3, b3, offs, out):
                                     p_f32[:, b * PAIRS : (b + 1) * PAIRS],
                                     COPY,
                                     scale=1.0 / O,
-                                    accum_out=p_mean[:, first_scene + b : first_scene + b + 1],
+                                    accum_out=p_mean[:, cut_first - first + b : cut_first - first + b + 1],
                                 )
-                    for m in range(KB):
-                        nc.tensor.matmul(
-                            pre[m][:].rearrange("p (b o) -> p b o", o=O),
-                            wb_bf16[layer][:, k, m * P : (m + 1) * P],
-                            p_mean[:].unsqueeze(2).to_broadcast([P, PIECE_SCENES, O]),
-                            start=False,
-                            stop=(k == KB - 1),
-                        )
+                    for part_first, part_scenes, pre in parts:
+                        for m in range(KB):
+                            nc.tensor.matmul(
+                                pre[:, m, :].rearrange("p (b o) -> p b o", o=O),
+                                wb_bf16[layer][:, k, m * P : (m + 1) * P],
+                                p_mean[:, part_first - first : part_first - first + part_scenes]
+                                .unsqueeze(2)
+                                .to_broadcast([P, part_scenes, O]),
+                                start=False,
+                                stop=(k == KB - 1 and m == KB - 1),
+                            )
 
-                    if x1_to_repeat:
-                        x1_piece, x1 = x1_to_repeat
-                        x_k = x_pool.tile([P, PIECE], F32, name=f"x_of_entry{k}")
+                    if to_repeat:
+                        x_k = x_pool.tile([P, LOOKUP * PAIRS], F32, name=f"x_of_entry{k}")
                         x_k_by_i = x_k[:].rearrange("p (b i o) -> p b i o", i=O, o=O)
-                        nc.scalar.copy(
-                            x_k_by_i[:, :, 0:SCALAR_COPIES, :],
-                            x1[:, k, :]
-                            .rearrange("p (b o) -> p b o", o=O)
-                            .unsqueeze(2)
-                            .to_broadcast([P, PIECE_SCENES, SCALAR_COPIES, O]),
-                        )
+                        for part_first, x1 in to_repeat:
+                            part_in_x_k = slice(part_first % LOOKUP, part_first % LOOKUP + PART)
+                            nc.scalar.copy(
+                                x_k_by_i[:, part_in_x_k, 0:SCALAR_COPIES, :],
+                                x1[:, k, :]
+                                .rearrange("p (b o) -> p b o", o=O)
+                                .unsqueeze(2)
+                                .to_broadcast([P, PART, SCALAR_COPIES, O]),
+                            )
                         nc.sync.dma_start(
                             x_k_by_i[:, :, SCALAR_COPIES : 2 * SCALAR_COPIES, :],
                             x_k_by_i[:, :, 0:SCALAR_COPIES, :],
@@ -176,22 +187,24 @@ def tile_gcn_b_kernel(tc, table, x0, w0, b0, w1, b1, w2, b2, w3, b3, offs, out):
                             x_k_by_i[:, :, 2 * SCALAR_COPIES : O, :],
                             x_k_by_i[:, :, 0 : 2 * SCALAR_COPIES, :],
                         )
-                        x_of_entry[1, x1_piece, k] = x_k
+                        x_of_entry[1, to_repeat[0][0] // LOOKUP, k] = x_k
 
-                x_new = held.tile([P, KB, PIECE_T], F32, name=f"x{layer + 1}_f32_{piece}")
-                for m in range(KB):
-                    nc.scalar.activation(
-                        x_new[:, m, :], pre[m][:], TANH, bias=layer_bias[:, layer, m : m + 1]
-                    )
-                    if layer == 1:
+                to_repeat = []
+                for part_first, part_scenes, pre in parts:
+                    columns = part_scenes * O
+                    x_new = held.tile([P, KB, columns], F32, name=f"x{layer + 1}_f32_{part_first}")
+                    nc.scalar.activation(x_new[:], pre[:], TANH)
+                    if layer == 0:
+                        x_new_bf16 = held.tile([P, KB, columns], BF16, name=f"x1_bf16_{part_first}")
+                        nc.scalar.copy(x_new_bf16[:], x_new[:])
+                        next_f32.append(x_new)
+                        next_bf16.append(x_new_bf16)
+                        to_repeat.append((part_first, x_new))
+                    else:
                         nc.sync.dma_start(
-                            out[m * P : (m + 1) * P, piece * PIECE_T : (piece + 1) * PIECE_T],
-                            x_new[:, m, :],
+                            out.rearrange("(k p) t -> p k t", p=P)[
+                                :, :, part_first * O : part_first * O + columns
+                            ],
+                            x_new[:],
                         )
-                if layer == 0:
-                    x_new_bf16 = held.tile([P, KB, PIECE_T], BF16, name=f"x1_bf16_{piece}")
-                    nc.scalar.copy(x_new_bf16[:], x_new[:])
-                    next_f32.append(x_new)
-                    next_bf16.append(x_new_bf16)
-                x1_to_repeat = (piece, x_new) if layer == 0 else None
             x_f32, x_bf16 = next_f32, next_bf16

@@ -21,7 +21,7 @@ N = B * PAIRS
 LOOKUP = 8
 PART = 8
 TAIL = 2
-SCALAR_COPIES = 4
+SCALAR_COPIES = O // 2
 
 assert LOOKUP % PART == 0 and KB * PART * O <= 512 and TAIL < PART
 
@@ -180,12 +180,7 @@ def tile_gcn_b_kernel(tc, table, x0, w0, b0, w1, b1, w2, b2, w3, b3, offs, out):
                                 .to_broadcast([P, PART, SCALAR_COPIES, O]),
                             )
                         nc.sync.dma_start(
-                            x_k_by_i[:, :, SCALAR_COPIES : 2 * SCALAR_COPIES, :],
-                            x_k_by_i[:, :, 0:SCALAR_COPIES, :],
-                        )
-                        nc.sync.dma_start(
-                            x_k_by_i[:, :, 2 * SCALAR_COPIES : O, :],
-                            x_k_by_i[:, :, 0 : 2 * SCALAR_COPIES, :],
+                            x_k_by_i[:, :, SCALAR_COPIES:O, :], x_k_by_i[:, :, 0:SCALAR_COPIES, :]
                         )
                         x_of_entry[1, to_repeat[0][0] // LOOKUP, k] = x_k
 

@@ -21,7 +21,6 @@ N = B * PAIRS
 LOOKUP = 8
 PART = 8
 TAIL = 2
-SCALAR_COPIES = O // 2
 
 assert LOOKUP % PART == 0 and KB * PART * O <= 512 and TAIL < PART
 
@@ -171,17 +170,13 @@ def tile_gcn_b_kernel(tc, table, x0, w0, b0, w1, b1, w2, b2, w3, b3, offs, out):
                         x_k = x_pool.tile([P, LOOKUP * PAIRS], F32, name=f"x_of_entry{k}")
                         x_k_by_i = x_k[:].rearrange("p (b i o) -> p b i o", i=O, o=O)
                         for part_first, x1 in to_repeat:
-                            part_in_x_k = slice(part_first % LOOKUP, part_first % LOOKUP + PART)
                             nc.scalar.copy(
-                                x_k_by_i[:, part_in_x_k, 0:SCALAR_COPIES, :],
+                                x_k_by_i[:, part_first % LOOKUP : part_first % LOOKUP + PART, :, :],
                                 x1[:, k, :]
                                 .rearrange("p (b o) -> p b o", o=O)
                                 .unsqueeze(2)
-                                .to_broadcast([P, PART, SCALAR_COPIES, O]),
+                                .to_broadcast([P, PART, O, O]),
                             )
-                        nc.sync.dma_start(
-                            x_k_by_i[:, :, SCALAR_COPIES:O, :], x_k_by_i[:, :, 0:SCALAR_COPIES, :]
-                        )
                         x_of_entry[1, to_repeat[0][0] // LOOKUP, k] = x_k
 
                 to_repeat = []

@@ -166,20 +166,21 @@ def tile_gcn_b_kernel(tc, table, x0, w0, b0, w1, b1, w2, b2, w3, b3, offs, out):
                                 stop=(k == KB - 1 and m == KB - 1),
                             )
 
-                    if to_repeat:
-                        x_k = x_pool.tile([P, LOOKUP * PAIRS], F32, name=f"x_of_entry{k}")
+                    if to_repeat and k > 0:
+                        x1_first, x1_k, x1_parts = to_repeat.pop(0)
+                        x_k = x_pool.tile([P, LOOKUP * PAIRS], F32, name=f"x_of_entry{x1_k}")
                         x_k_by_i = x_k[:].rearrange("p (b i o) -> p b i o", i=O, o=O)
-                        for part_first, x1 in to_repeat:
+                        for part_first, x1 in x1_parts:
                             nc.scalar.copy(
                                 x_k_by_i[:, part_first % LOOKUP : part_first % LOOKUP + PART, :, :],
-                                x1[:, k, :]
+                                x1[:, x1_k, :]
                                 .rearrange("p (b o) -> p b o", o=O)
                                 .unsqueeze(2)
                                 .to_broadcast([P, PART, O, O]),
                             )
-                        x_of_entry[1, to_repeat[0][0] // LOOKUP, k] = x_k
+                        x_of_entry[1, x1_first // LOOKUP, x1_k] = x_k
 
-                to_repeat = []
+                x1_parts = []
                 for part_first, part_scenes, pre in parts:
                     columns = part_scenes * O
                     x_new = held.tile([P, KB, columns], F32, name=f"x{layer + 1}_f32_{part_first}")
@@ -189,7 +190,7 @@ def tile_gcn_b_kernel(tc, table, x0, w0, b0, w1, b1, w2, b2, w3, b3, offs, out):
                         nc.scalar.copy(x_new_bf16[:], x_new[:])
                         next_f32.append(x_new)
                         next_bf16.append(x_new_bf16)
-                        to_repeat.append((part_first, x_new))
+                        x1_parts.append((part_first, x_new))
                     else:
                         nc.sync.dma_start(
                             out.rearrange("(k p) t -> p k t", p=P)[
@@ -197,4 +198,6 @@ def tile_gcn_b_kernel(tc, table, x0, w0, b0, w1, b1, w2, b2, w3, b3, offs, out):
                             ],
                             x_new[:],
                         )
+                if layer == 0:
+                    to_repeat += [(first, k, x1_parts) for k in range(KB)]
             x_f32, x_bf16 = next_f32, next_bf16

@@ -19,17 +19,11 @@ T = B * O
 PAIRS = O * O
 N = B * PAIRS
 LOOKUP = 8
-PART = 8
 TAIL = 2
 
-assert LOOKUP % PART == 0 and KB * PART * O <= 512 and TAIL < PART
+assert KB * LOOKUP * O <= 512
 
 FLOPS = 2 * (2 * D * N + 2 * D * D * B + 2 * D * D * T)
-
-
-def cut(first, last, size):
-    starts = [b for b in range(first, last) if b == first or b % size == 0]
-    return [(b, end - b) for b, end in zip(starts, starts[1:] + [last])]
 
 
 def tile_gcn_b_kernel(tc, table, x0, w0, b0, w1, b1, w2, b2, w3, b3, offs, out):
@@ -40,7 +34,7 @@ def tile_gcn_b_kernel(tc, table, x0, w0, b0, w1, b1, w2, b2, w3, b3, offs, out):
         tc.tile_pool(name="products", bufs=4) as products,
         tc.tile_pool(name="unused", bufs=2) as unused,
         tc.tile_pool(name="sums", bufs=2 * KB) as sums,
-        tc.psum_pool(name="pre_psum", bufs=2) as pre_psum,
+        tc.psum_pool(name="pre_psum", bufs=3) as pre_psum,
     ):
         x_start = held.tile([P, KB, O], F32, name="x_start")
         nc.scalar.dma_start(x_start[:], x0.rearrange("(k p) o -> p k o", p=P))
@@ -83,34 +77,34 @@ def tile_gcn_b_kernel(tc, table, x0, w0, b0, w1, b1, w2, b2, w3, b3, offs, out):
             )
             for i in range(B // LOOKUP):
                 x_of_entry[0, i, k] = x_k
-        x0_f32 = held.tile([P, KB, PART * O], F32, name="x0_f32")
+        x0_f32 = held.tile([P, KB, LOOKUP * O], F32, name="x0_f32")
         nc.scalar.copy(
             x0_f32[:].rearrange("p k (b o) -> p k b o", o=O),
-            x_start[:].unsqueeze(2).to_broadcast([P, KB, PART, O]),
+            x_start[:].unsqueeze(2).to_broadcast([P, KB, LOOKUP, O]),
         )
-        x0_bf16 = held.tile([P, KB, PART * O], BF16, name="x0_bf16")
+        x0_bf16 = held.tile([P, KB, LOOKUP * O], BF16, name="x0_bf16")
         nc.scalar.copy(x0_bf16[:], x0_f32[:])
 
-        x_f32 = [x0_f32] * (B // PART)
-        x_bf16 = [x0_bf16] * (B // PART)
+        x_f32 = [x0_f32] * (B // LOOKUP)
+        x_bf16 = [x0_bf16] * (B // LOOKUP)
         to_repeat = []
         for layer in range(2):
-            pieces = cut(0, B, LOOKUP)
+            pieces = [(first, LOOKUP) for first in range(0, B, LOOKUP)]
             if layer == 1:
                 pieces[-1:] = [(B - LOOKUP, LOOKUP - TAIL), (B - TAIL, TAIL)]
+            look_ups = [(first, scenes, k) for first, scenes in pieces for k in range(KB)]
+            if layer == 0:
+                look_ups.insert(1, look_ups.pop(KB))
             next_f32, next_bf16 = [], []
-            for first, scenes in pieces:
-                parts = []
-                for part_first, part_scenes in cut(first, first + scenes, PART):
-                    columns = part_scenes * O
-                    x_columns = slice(part_first % PART * O, part_first % PART * O + columns)
+            pres = {}
+            for first, scenes, k in look_ups:
+                columns = scenes * O
+                if k == 0:
+                    x_columns = slice(first % LOOKUP * O, first % LOOKUP * O + columns)
                     pre = pre_psum.tile([P, KB, columns], F32, name="pre")
+                    pres[first] = pre
                     nc.tensor.matmul(
-                        pre[:],
-                        identity_f32[:],
-                        x_f32[part_first // PART][:, :, x_columns],
-                        start=True,
-                        stop=False,
+                        pre[:], identity_f32[:], x_f32[first // LOOKUP][:, :, x_columns], start=True, stop=False
                     )
                     nc.tensor.matmul(
                         pre[:],
@@ -124,80 +118,69 @@ def tile_gcn_b_kernel(tc, table, x0, w0, b0, w1, b1, w2, b2, w3, b3, offs, out):
                             nc.tensor.matmul(
                                 pre[:, m, :],
                                 wa_bf16[layer][:, k_in, m * P : (m + 1) * P],
-                                x_bf16[part_first // PART][:, k_in, x_columns],
+                                x_bf16[first // LOOKUP][:, k_in, x_columns],
                                 start=False,
                                 stop=False,
                             )
-                    parts.append((part_first, part_scenes, pre))
+                pre = pres[first]
 
-                for k in range(KB):
-                    is_last = layer == 1 and first == B - TAIL and k == KB - 1
-                    p_mean = sums.tile([P, scenes], BF16, name="p_mean")
-                    for cut_first, cut_scenes in cut(first, first + scenes, 1 if is_last else LOOKUP):
-                        x_first = cut_first % LOOKUP * PAIRS
-                        p_f32 = products.tile([P, cut_scenes * PAIRS], F32, name="p_f32")
-                        nc.vector.tensor_tensor(
-                            p_f32[:],
-                            tables[k][:].indirect(
-                                offsets[:, cut_first * PAIRS // 16 : (cut_first + cut_scenes) * PAIRS // 16]
-                            ),
-                            x_of_entry[layer, first // LOOKUP, k][:, x_first : x_first + cut_scenes * PAIRS],
-                            MULT,
-                        )
-                        for b in range(cut_scenes):
-                            unused_copy = unused.tile([P, PAIRS], BF16, name="unused_copy")
-                            with nc.allow_low_precision(reason="the sum is a bfloat16 matmul's operand"):
-                                nc.scalar.activation(
-                                    unused_copy[:],
-                                    p_f32[:, b * PAIRS : (b + 1) * PAIRS],
-                                    COPY,
-                                    scale=1.0 / O,
-                                    accum_out=p_mean[:, cut_first - first + b : cut_first - first + b + 1],
-                                )
-                    for part_first, part_scenes, pre in parts:
-                        for m in range(KB):
-                            nc.tensor.matmul(
-                                pre[:, m, :].rearrange("p (b o) -> p b o", o=O),
-                                wb_bf16[layer][:, k, m * P : (m + 1) * P],
-                                p_mean[:, part_first - first : part_first - first + part_scenes]
-                                .unsqueeze(2)
-                                .to_broadcast([P, part_scenes, O]),
-                                start=False,
-                                stop=(k == KB - 1 and m == KB - 1),
+                is_last = layer == 1 and first == B - TAIL and k == KB - 1
+                cut_scenes = 1 if is_last else scenes
+                p_mean = sums.tile([P, scenes], BF16, name="p_mean")
+                for cut in range(first, first + scenes, cut_scenes):
+                    x_first = cut % LOOKUP * PAIRS
+                    p_f32 = products.tile([P, cut_scenes * PAIRS], F32, name="p_f32")
+                    nc.vector.tensor_tensor(
+                        p_f32[:],
+                        tables[k][:].indirect(
+                            offsets[:, cut * PAIRS // 16 : (cut + cut_scenes) * PAIRS // 16]
+                        ),
+                        x_of_entry[layer, first // LOOKUP, k][:, x_first : x_first + cut_scenes * PAIRS],
+                        MULT,
+                    )
+                    for b in range(cut_scenes):
+                        unused_copy = unused.tile([P, PAIRS], BF16, name="unused_copy")
+                        with nc.allow_low_precision(reason="the sum is a bfloat16 matmul's operand"):
+                            nc.scalar.activation(
+                                unused_copy[:],
+                                p_f32[:, b * PAIRS : (b + 1) * PAIRS],
+                                COPY,
+                                scale=1.0 / O,
+                                accum_out=p_mean[:, cut - first + b : cut - first + b + 1],
                             )
+                for m in range(KB):
+                    nc.tensor.matmul(
+                        pre[:, m, :].rearrange("p (b o) -> p b o", o=O),
+                        wb_bf16[layer][:, k, m * P : (m + 1) * P],
+                        p_mean[:].unsqueeze(2).to_broadcast([P, scenes, O]),
+                        start=False,
+                        stop=(k == KB - 1 and m == KB - 1),
+                    )
 
-                    if to_repeat and k > 0:
-                        x1_first, x1_k, x1_parts = to_repeat.pop(0)
-                        x_k = x_pool.tile([P, LOOKUP * PAIRS], F32, name=f"x_of_entry{x1_k}")
-                        x_k_by_i = x_k[:].rearrange("p (b i o) -> p b i o", i=O, o=O)
-                        for part_first, x1 in x1_parts:
-                            nc.scalar.copy(
-                                x_k_by_i[:, part_first % LOOKUP : part_first % LOOKUP + PART, :, :],
-                                x1[:, x1_k, :]
-                                .rearrange("p (b o) -> p b o", o=O)
-                                .unsqueeze(2)
-                                .to_broadcast([P, PART, O, O]),
-                            )
-                        x_of_entry[1, x1_first // LOOKUP, x1_k] = x_k
+                if to_repeat and k > 0:
+                    i, x1_k, x1 = to_repeat.pop(0)
+                    x_k = x_pool.tile([P, LOOKUP * PAIRS], F32, name=f"x_of_entry{x1_k}")
+                    nc.scalar.copy(
+                        x_k[:].rearrange("p (b i o) -> p b i o", i=O, o=O),
+                        x1[:, x1_k, :]
+                        .rearrange("p (b o) -> p b o", o=O)
+                        .unsqueeze(2)
+                        .to_broadcast([P, LOOKUP, O, O]),
+                    )
+                    x_of_entry[1, i, x1_k] = x_k
 
-                x1_parts = []
-                for part_first, part_scenes, pre in parts:
-                    columns = part_scenes * O
-                    x_new = held.tile([P, KB, columns], F32, name=f"x{layer + 1}_f32_{part_first}")
+                if k == KB - 1:
+                    x_new = held.tile([P, KB, columns], F32, name=f"x{layer + 1}_f32_{first}")
                     nc.scalar.activation(x_new[:], pre[:], TANH)
                     if layer == 0:
-                        x_new_bf16 = held.tile([P, KB, columns], BF16, name=f"x1_bf16_{part_first}")
+                        x_new_bf16 = held.tile([P, KB, columns], BF16, name=f"x1_bf16_{first}")
                         nc.scalar.copy(x_new_bf16[:], x_new[:])
                         next_f32.append(x_new)
                         next_bf16.append(x_new_bf16)
-                        x1_parts.append((part_first, x_new))
+                        to_repeat += [(first // LOOKUP, block, x_new) for block in range(KB)]
                     else:
                         nc.sync.dma_start(
-                            out.rearrange("(k p) t -> p k t", p=P)[
-                                :, :, part_first * O : part_first * O + columns
-                            ],
+                            out.rearrange("(k p) t -> p k t", p=P)[:, :, first * O : first * O + columns],
                             x_new[:],
                         )
-                if layer == 0:
-                    to_repeat += [(first, k, x1_parts) for k in range(KB)]
             x_f32, x_bf16 = next_f32, next_bf16

@@ -37,19 +37,19 @@ def tile_gcn_b_kernel(tc, table, x0, w0, b0, w1, b1, w2, b2, w3, b3, offs, out):
         tc.psum_pool(name="pre_psum", bufs=3) as pre_psum,
     ):
         x_start = held.tile([P, KB, O], F32, name="x_start")
-        nc.scalar.dma_start(x_start[:], x0.rearrange("(k p) o -> p k o", p=P))
+        nc.sync.dma_start(x_start[:], x0.rearrange("(k p) o -> p k o", p=P))
         offsets = held.tile([P, N // 16], U16, name="offsets")
         nc.sync.dma_start(offsets[:], offs)
+        tables = [held.tile([P, S], F32, name=f"table{k}") for k in range(KB)]
+        nc.sync.dma_start(tables[0][:, 0 : S // 2], table[0:P, 0 : S // 2])
+        nc.scalar.dma_start(tables[0][:, S // 2 : S], table[0:P, S // 2 : S])
+        for k in range(1, KB):
+            nc.sync.dma_start(tables[k][:], table[k * P : (k + 1) * P, :])
         bias_rows = held.tile([4 * KB, P], F32, name="bias_rows")
         for i, b in enumerate((b0, b1, b2, b3)):
             nc.scalar.dma_start(
                 bias_rows[i * KB : (i + 1) * KB, :], b.rearrange("(k p) one -> k (p one)", p=P)
             )
-        tables = []
-        for k in range(KB):
-            table_k = held.tile([P, S], F32, name=f"table{k}")
-            nc.sync.dma_start(table_k[:], table[k * P : (k + 1) * P, :])
-            tables.append(table_k)
         wa_bf16, wb_bf16 = [], []
         for layer, (wa, wb) in enumerate(((w0, w1), (w2, w3))):
             wb_tile = held.tile([P, KB, D], BF16, name=f"wb{layer}_bf16")

@@ -43,13 +43,13 @@ def tile_gcn_b_kernel(tc, table, x0, w0, b0, w1, b1, w2, b2, w3, b3, offs, out):
         tables = [held.tile([P, S], F32, name=f"table{k}") for k in range(KB)]
         nc.sync.dma_start(tables[0][:, 0 : S // 2], table[0:P, 0 : S // 2])
         nc.scalar.dma_start(tables[0][:, S // 2 : S], table[0:P, S // 2 : S])
-        for k in range(1, KB):
-            nc.sync.dma_start(tables[k][:], table[k * P : (k + 1) * P, :])
         bias_rows = held.tile([4 * KB, P], F32, name="bias_rows")
         for i, b in enumerate((b0, b1, b2, b3)):
-            nc.scalar.dma_start(
+            nc.sync.dma_start(
                 bias_rows[i * KB : (i + 1) * KB, :], b.rearrange("(k p) one -> k (p one)", p=P)
             )
+        for k in range(1, KB):
+            nc.sync.dma_start(tables[k][:], table[k * P : (k + 1) * P, :])
         wa_bf16, wb_bf16 = [], []
         for layer, (wa, wb) in enumerate(((w0, w1), (w2, w3))):
             wb_tile = held.tile([P, KB, D], BF16, name=f"wb{layer}_bf16")
@@ -71,7 +71,8 @@ def tile_gcn_b_kernel(tc, table, x0, w0, b0, w1, b1, w2, b2, w3, b3, offs, out):
         x_of_entry = {}
         for k in range(KB):
             x_k = x_pool.tile([P, LOOKUP * PAIRS], F32, name=f"x_of_entry{k}")
-            nc.scalar.copy(
+            copy = nc.vector.tensor_copy if k == 0 else nc.scalar.copy
+            copy(
                 x_k[:].rearrange("p (g o) -> p g o", o=O),
                 x_start[:, k, :].unsqueeze(1).to_broadcast([P, LOOKUP * O, O]),
             )

@@ -37,12 +37,14 @@ def tile_gcn_b_kernel(tc, table, x0, w0, b0, w1, b1, w2, b2, w3, b3, offs, out):
         tc.psum_pool(name="pre_psum", bufs=3) as pre_psum,
     ):
         x_start = held.tile([P, KB, O], F32, name="x_start")
-        nc.sync.dma_start(x_start[:], x0.rearrange("(k p) o -> p k o", p=P))
+        x0_by_block = x0.rearrange("(k p) o -> p k o", p=P)
+        nc.sync.dma_start(x_start[:, 0, :], x0_by_block[:, 0, :])
         offsets = held.tile([P, N // 16], U16, name="offsets")
         nc.sync.dma_start(offsets[:], offs)
         tables = [held.tile([P, S], F32, name=f"table{k}") for k in range(KB)]
         nc.sync.dma_start(tables[0][:, 0 : S // 2], table[0:P, 0 : S // 2])
         nc.scalar.dma_start(tables[0][:, S // 2 : S], table[0:P, S // 2 : S])
+        nc.sync.dma_start(x_start[:, 1:KB, :], x0_by_block[:, 1:KB, :])
         bias_rows = held.tile([4 * KB, P], F32, name="bias_rows")
         for i, b in enumerate((b0, b1, b2, b3)):
             nc.sync.dma_start(

@@ -31,7 +31,7 @@ def tile_gcn_b_kernel(tc, table, x0, w0, b0, w1, b1, w2, b2, w3, b3, offs, out):
     with (
         tc.tile_pool(name="held", bufs=1) as held,
         tc.tile_pool(name="x_pool", bufs=2) as x_pool,
-        tc.tile_pool(name="products", bufs=4) as products,
+        tc.tile_pool(name="products", bufs=6) as products,
         tc.tile_pool(name="unused", bufs=2) as unused,
         tc.tile_pool(name="sums", bufs=2 * KB) as sums,
         tc.psum_pool(name="pre_psum", bufs=3) as pre_psum,
@@ -182,7 +182,8 @@ def tile_gcn_b_kernel(tc, table, x0, w0, b0, w1, b1, w2, b2, w3, b3, offs, out):
                         next_bf16.append(x_new_bf16)
                         to_repeat += [(first // LOOKUP, block, x_new) for block in range(KB)]
                     else:
-                        nc.sync.dma_start(
+                        queue = nc.scalar if first == B - TAIL else nc.sync
+                        queue.dma_start(
                             out.rearrange("(k p) t -> p k t", p=P)[:, :, first * O : first * O + columns],
                             x_new[:],
                         )

import concourse.mybir as mybir
from concourse.masks import make_identity

F32 = mybir.dt.float32
BF16 = mybir.dt.bfloat16
U16 = mybir.dt.uint16
MULT = mybir.AluOpType.mult
ADD = mybir.AluOpType.add
TANH = mybir.ActivationFunctionType.Tanh
COPY = mybir.ActivationFunctionType.Copy

P = 128
D = 512
KB = D // P
S = 4096
B = 24
O = 16
T = B * O
PAIRS = O * O
N = B * PAIRS
LOOKUP = 8
TAIL = 2

assert KB * LOOKUP * O <= 512

FLOPS = 2 * (2 * D * N + 2 * D * D * B + 2 * D * D * T)


def tile_gcn_b_kernel(tc, table, x0, w0, b0, w1, b1, w2, b2, w3, b3, offs, out):
    nc = tc.nc
    with (
        tc.tile_pool(name="held", bufs=1) as held,
        tc.tile_pool(name="x_pool", bufs=2) as x_pool,
        tc.tile_pool(name="products", bufs=6) as products,
        tc.tile_pool(name="unused", bufs=2) as unused,
        tc.tile_pool(name="sums", bufs=2 * KB) as sums,
        tc.psum_pool(name="pre_psum", bufs=3) as pre_psum,
    ):
        x_start = held.tile([P, KB, O], F32, name="x_start")
        x0_by_block = x0.rearrange("(k p) o -> p k o", p=P)
        nc.sync.dma_start(x_start[:, 0, :], x0_by_block[:, 0, :])
        offsets = held.tile([P, N // 16], U16, name="offsets")
        nc.sync.dma_start(offsets[:], offs)
        tables = [held.tile([P, S], F32, name=f"table{k}") for k in range(KB)]
        nc.sync.dma_start(tables[0][:, 0 : S // 2], table[0:P, 0 : S // 2])
        nc.scalar.dma_start(tables[0][:, S // 2 : S], table[0:P, S // 2 : S])
        nc.sync.dma_start(x_start[:, 1:KB, :], x0_by_block[:, 1:KB, :])
        bias_rows = held.tile([4 * KB, P], F32, name="bias_rows")
        for i, b in enumerate((b0, b1, b2, b3)):
            nc.sync.dma_start(
                bias_rows[i * KB : (i + 1) * KB, :], b.rearrange("(k p) one -> k (p one)", p=P)
            )
        for k in range(1, KB):
            nc.sync.dma_start(tables[k][:], table[k * P : (k + 1) * P, :])
        wa_bf16, wb_bf16 = [], []
        for layer, (wa, wb) in enumerate(((w0, w1), (w2, w3))):
            wb_tile = held.tile([P, KB, D], BF16, name=f"wb{layer}_bf16")
            nc.sync.dma_start(wb_tile[:], wb.rearrange("(k p) m -> p k m", p=P))
            wb_bf16.append(wb_tile)
            wa_tile = held.tile([P, KB, D], BF16, name=f"wa{layer}_bf16")
            nc.sync.dma_start(wa_tile[:], wa.rearrange("(k p) m -> p k m", p=P))
            wa_bf16.append(wa_tile)

        identity_f32 = held.tile([P, P], F32, name="identity_f32")
        make_identity(nc, identity_f32[:])

        row_is = identity_f32[0 : 4 * KB, 0 : 4 * KB].rearrange("r (l i k) -> r l i k", l=2, i=2)
        bb_weight = held.tile([4 * KB, 2, KB], F32, name="bb_weight")
        nc.gpsimd.tensor_scalar(bb_weight[:], row_is[:, :, 1, :], float(PAIRS // O), None, MULT)
        combine = held.tile([4 * KB, 2, KB], F32, name="combine")
        nc.gpsimd.tensor_tensor(combine[:], bb_weight[:], row_is[:, :, 0, :], ADD)

        x_of_entry = {}
        for k in range(KB):
            x_k = x_pool.tile([P, LOOKUP * PAIRS], F32, name=f"x_of_entry{k}")
            copy = nc.vector.tensor_copy if k == 0 else nc.scalar.copy
            copy(
                x_k[:].rearrange("p (g o) -> p g o", o=O),
                x_start[:, k, :].unsqueeze(1).to_broadcast([P, LOOKUP * O, O]),
            )
            for i in range(B // LOOKUP):
                x_of_entry[0, i, k] = x_k
        x0_f32 = held.tile([P, KB, LOOKUP * O], F32, name="x0_f32")
        nc.scalar.copy(
            x0_f32[:].rearrange("p k (b o) -> p k b o", o=O),
            x_start[:].unsqueeze(2).to_broadcast([P, KB, LOOKUP, O]),
        )
        x0_bf16 = held.tile([P, KB, LOOKUP * O], BF16, name="x0_bf16")
        nc.scalar.copy(x0_bf16[:], x0_f32[:])

        x_f32 = [x0_f32] * (B // LOOKUP)
        x_bf16 = [x0_bf16] * (B // LOOKUP)
        to_repeat = []
        for layer in range(2):
            pieces = [(first, LOOKUP) for first in range(0, B, LOOKUP)]
            if layer == 1:
                pieces[-1:] = [(B - LOOKUP, LOOKUP - TAIL), (B - TAIL, TAIL)]
            look_ups = [(first, scenes, k) for first, scenes in pieces for k in range(KB)]
            if layer == 0:
                look_ups.insert(1, look_ups.pop(KB))
            next_f32, next_bf16 = [], []
            pres = {}
            for first, scenes, k in look_ups:
                columns = scenes * O
                if k == 0:
                    x_columns = slice(first % LOOKUP * O, first % LOOKUP * O + columns)
                    pre = pre_psum.tile([P, KB, columns], F32, name="pre")
                    pres[first] = pre
                    nc.tensor.matmul(
                        pre[:], identity_f32[:], x_f32[first // LOOKUP][:, :, x_columns], start=True, stop=False
                    )
                    nc.tensor.matmul(
                        pre[:],
                        bias_rows[:],
                        combine[:, layer, :].unsqueeze(2).to_broadcast([4 * KB, KB, columns]),
                        start=False,
                        stop=False,
                    )
                    for m in range(KB):
                        for k_in in range(KB):
                            nc.tensor.matmul(
                                pre[:, m, :],
                                wa_bf16[layer][:, k_in, m * P : (m + 1) * P],
                                x_bf16[first // LOOKUP][:, k_in, x_columns],
                                start=False,
                                stop=False,
                            )
                pre = pres[first]

                is_last = layer == 1 and first == B - TAIL and k == KB - 1
                cut_scenes = 1 if is_last else scenes
                p_mean = sums.tile([P, scenes], BF16, name="p_mean")
                for cut in range(first, first + scenes, cut_scenes):
                    x_first = cut % LOOKUP * PAIRS
                    p_f32 = products.tile([P, cut_scenes * PAIRS], F32, name="p_f32")
                    nc.vector.tensor_tensor(
                        p_f32[:],
                        tables[k][:].indirect(
                            offsets[:, cut * PAIRS // 16 : (cut + cut_scenes) * PAIRS // 16]
                        ),
                        x_of_entry[layer, first // LOOKUP, k][:, x_first : x_first + cut_scenes * PAIRS],
                        MULT,
                    )
                    for b in range(cut_scenes):
                        unused_copy = unused.tile([P, PAIRS], BF16, name="unused_copy")
                        with nc.allow_low_precision(reason="the sum is a bfloat16 matmul's operand"):
                            nc.scalar.activation(
                                unused_copy[:],
                                p_f32[:, b * PAIRS : (b + 1) * PAIRS],
                                COPY,
                                scale=1.0 / O,
                                accum_out=p_mean[:, cut - first + b : cut - first + b + 1],
                            )
                for m in range(KB):
                    nc.tensor.matmul(
                        pre[:, m, :].rearrange("p (b o) -> p b o", o=O),
                        wb_bf16[layer][:, k, m * P : (m + 1) * P],
                        p_mean[:].unsqueeze(2).to_broadcast([P, scenes, O]),
                        start=False,
                        stop=(k == KB - 1 and m == KB - 1),
                    )

                if to_repeat and k > 0:
                    i, x1_k, x1 = to_repeat.pop(0)
                    x_k = x_pool.tile([P, LOOKUP * PAIRS], F32, name=f"x_of_entry{x1_k}")
                    nc.scalar.copy(
                        x_k[:].rearrange("p (b i o) -> p b i o", i=O, o=O),
                        x1[:, x1_k, :]
                        .rearrange("p (b o) -> p b o", o=O)
                        .unsqueeze(2)
                        .to_broadcast([P, LOOKUP, O, O]),
                    )
                    x_of_entry[1, i, x1_k] = x_k

                if k == KB - 1:
                    x_new = held.tile([P, KB, columns], F32, name=f"x{layer + 1}_f32_{first}")
                    nc.scalar.activation(x_new[:], pre[:], TANH)
                    if layer == 0:
                        x_new_bf16 = held.tile([P, KB, columns], BF16, name=f"x1_bf16_{first}")
                        nc.scalar.copy(x_new_bf16[:], x_new[:])
                        next_f32.append(x_new)
                        next_bf16.append(x_new_bf16)
                        to_repeat += [(first // LOOKUP, block, x_new) for block in range(KB)]
                    else:
                        queue = nc.scalar if first == B - TAIL else nc.sync
                        queue.dma_start(
                            out.rearrange("(k p) t -> p k t", p=P)[:, :, first * O : first * O + columns],
                            x_new[:],
                        )
            x_f32, x_bf16 = next_f32, next_bf16
